import numpy as np
import ml_dtypes


def mxq(x, axis, fmt="e4m3"):
    dtype, down = {"e4m3": (ml_dtypes.float8_e4m3fn, 7), "e5m2": (ml_dtypes.float8_e5m2, 14)}[fmt]
    v = np.moveaxis(np.asarray(x, np.float32).astype(ml_dtypes.bfloat16).astype(np.float64), axis, -1)
    blocks = v.reshape(v.shape[:-1] + (-1, 32))
    amax = np.abs(blocks).max(-1, keepdims=True)
    byte = np.maximum(np.where(amax > 0, np.frexp(amax)[1] - 1 + 127, 0) - down, 1)
    scale = np.exp2(byte - 127.0)
    codes = (blocks / scale).astype(np.float32).astype(dtype).astype(np.float64)
    return np.moveaxis((codes * scale).reshape(v.shape), -1, axis)


WIDE = False


def mx_kscale(k):
    if not WIDE:
        return np.ones(k)
    levels = np.array([10, -10, 5, -5, 0])
    a = np.random.permutation(np.resize(levels, k // 512 * 4)).reshape(k // 512, 4)
    idx = np.arange(k)
    return np.exp2(a[idx // 512, idx % 128 // 32])


BF16 = ml_dtypes.bfloat16


def bf(x):
    return np.asarray(x, np.float32).astype(BF16)


def f64(x):
    return np.asarray(x).astype(np.float64)


B, W, MID = 512, 1024, 2048


def setup_inputs():
    s, t = mx_kscale(MID), mx_kscale(MID)
    return {"h3": bf(np.maximum(np.random.standard_normal((B, MID)), 0.0) * np.sqrt(2.0) * s),
            "w4": bf(np.random.standard_normal((MID, MID)) * np.sqrt(2.0 / MID) / s[:, None] * t),
            "b4": bf(np.random.standard_normal(MID) * 0.1 * t),
            "w5": bf(np.random.standard_normal((MID, W)) * 0.7 / np.sqrt(MID) / t[:, None]),
            "b5": bf(np.random.standard_normal(W) * 0.2),
            "x": bf(np.random.standard_normal((B, W))),
            "log_det_J": bf(np.random.standard_normal(B) * 0.1 * np.sqrt(W))}


def reference(h3, w4, b4, w5, b5, x, log_det_J):
    xf = f64(x)
    x1 = xf[:, 0::2]
    x2 = xf[:, 1::2]
    h4 = np.maximum((mxq(f64(h3), 1, "e4m3") @ mxq(f64(w4), 0, "e4m3")) + f64(b4), 0.0)
    bvec = (mxq(h4, 1, "e4m3") @ mxq(f64(w5), 0, "e4m3")) + f64(b5)
    b1t = np.tanh(bvec[:, 0::2])
    b2t = bvec[:, 1::2]
    y2 = x2 * np.exp(b1t) + b2t
    log_det = f64(log_det_J) + np.sum(b1t, axis=1)
    y = np.stack((x1, y2), axis=2).reshape(xf.shape)
    return (y, log_det)

@@ -1,0 +1,286 @@
+from contextlib import ExitStack
+
+import concourse.mybir as mybir
+from concourse.masks import make_identity
+
+F32 = mybir.dt.float32
+BF16 = mybir.dt.bfloat16
+U32 = mybir.dt.uint32
+U8 = mybir.dt.uint8
+FP8X4 = mybir.dt.float8_e4m3fn_x4
+ACT = mybir.ActivationFunctionType
+ALU = mybir.AluOpType
+
+BATCH, MID, WIDTH = 512, 2048, 1024
+FLOPS = 2 * BATCH * MID * MID + 2 * BATCH * MID * WIDTH
+
+P = 128
+PACK = 4
+K_PASS = P * PACK
+PASSES = MID // K_PASS
+BATCH_TILES = BATCH // P
+BANK = 512
+BANKS = 8
+CHUNK = 1024
+PAIRS = BANK // 2
+RUN = 4
+LOADS_AHEAD = 5
+
+
+def regroup(nc, grouped, planes):
+    width = planes.shape[2]
+    half = width // 2
+    nc.vector.tensor_copy(
+        out=grouped[:, 0:half, :].rearrange("p (c i) t -> p c t i", i=RUN),
+        in_=planes[:, :, 0:half].rearrange("p t (c i) -> p c t i", i=RUN),
+    )
+    nc.scalar.copy(
+        out=grouped[:, half:width, :].rearrange("p (c i) t -> p c t i", i=RUN),
+        in_=planes[:, :, half:width].rearrange("p t (c i) -> p c t i", i=RUN),
+    )
+
+
+def quantise(nc, codes, scales, grouped):
+    nc.vector.quantize_mx(
+        out=codes.bitcast(FP8X4),
+        scales=scales,
+        in_=grouped.rearrange("p w t -> p (w t)"),
+    )
+
+
+def tile_affinecoupling_pa_kernel(tc, h3, w4, b4, w5, b5, x, log_det_J, out_0, out_1):
+    nc = tc.nc
+    with ExitStack() as ctx:
+        ctx.enter_context(tc.manual_schedule())
+        const = ctx.enter_context(tc.tile_pool(name="const", bufs=1))
+        raw_pool = ctx.enter_context(tc.tile_pool(name="raw", bufs=LOADS_AHEAD + 2))
+        grouped_pool = ctx.enter_context(tc.tile_pool(name="grouped", bufs=4))
+        weight_pool = ctx.enter_context(tc.tile_pool(name="weight", bufs=5))
+        tail_pool = ctx.enter_context(tc.tile_pool(name="tail", bufs=3))
+        psum = ctx.enter_context(tc.psum_pool(name="psum", bufs=1))
+
+        def bank(i, shape, dtype):
+            return psum.tile(shape, dtype, name="bank%d" % i)
+
+        ident_f32 = const.tile([P, P], F32)
+        make_identity(nc, ident_f32[:])
+        ident_bf16 = const.tile([P, P], BF16)
+        make_identity(nc, ident_bf16[:])
+
+        warm = const.tile([P, 1], F32)
+        nc.vector.memset(warm[:], 0.0)
+        nc.scalar.activation(out=warm[:], in_=warm[:], func=ACT.Tanh)
+
+        b4_rows = const.tile([P, P], BF16)
+        nc.vector.memset(b4_rows[:], 0.0)
+        nc.scalar.dma_start(out=b4_rows[0 : MID // P, :], in_=b4.rearrange("(c p) -> c p", p=P))
+        ldj_rows = const.tile([P, P], BF16)
+        nc.vector.memset(ldj_rows[:], 0.0)
+        nc.scalar.dma_start(
+            out=ldj_rows[0:BATCH_TILES, :], in_=log_det_J.rearrange("(s p) -> s p", p=P)
+        )
+        ld_cols = const.tile([P, P], F32)
+        nc.vector.memset(ld_cols[:], 0.0)
+
+        h3_raw = const.tile([P, BATCH_TILES, MID], BF16)
+        for s in range(BATCH_TILES):
+            nc.sync.dma_start(out=h3_raw[:, s, :], in_=h3[s * P : (s + 1) * P, :])
+
+        x_sb = const.tile([P, BATCH_TILES, WIDTH], BF16)
+        b5_all = const.tile([P, WIDTH], BF16)
+
+        chunk_rows = []
+        for half in range(2):
+            for g in range(PASSES):
+                rows = w4[g * K_PASS : (g + 1) * K_PASS, half * CHUNK : (half + 1) * CHUNK]
+                chunk_rows.append(rows.rearrange("(p t) n -> p t n", t=PACK))
+        for r in range(PASSES):
+            rows = w5[r * K_PASS : (r + 1) * K_PASS, :]
+            chunk_rows.append(rows.rearrange("(t p) n -> p t n", p=P))
+        chunks = len(chunk_rows)
+        raw_tiles, grouped_tiles = [], []
+
+        def load(j):
+            if j == 2 * PASSES:
+                nc.sync.dma_start(out=x_sb[:], in_=x.rearrange("(s p) w -> p s w", p=P))
+                nc.sync.dma_start(out=b5_all[:], in_=b5.partition_broadcast(P))
+            raw = raw_pool.tile([P, PACK, CHUNK], BF16)
+            nc.sync.dma_start(out=raw[:], in_=chunk_rows[j])
+            raw_tiles.append(raw)
+
+        def fill(j):
+            grouped = grouped_pool.tile([P, CHUNK, PACK], BF16, align_bytes=64)
+            regroup(nc, grouped, raw_tiles[j])
+            grouped_tiles.append(grouped)
+
+        def quantise_chunk(j):
+            w_codes = weight_pool.tile([P, CHUNK], U32, align_bytes=64)
+            w_scales = weight_pool.tile([P, CHUNK], U8, align_bytes=64)
+            for cols in (slice(0, BANK), slice(BANK, CHUNK)):
+                quantise(nc, w_codes[:, cols], w_scales[:, cols], grouped_tiles[j][:, cols, :])
+            return w_codes, w_scales
+
+        for j in range(LOADS_AHEAD):
+            load(j)
+
+        h3_codes = const.tile([P, PASSES * BATCH], U32, align_bytes=64)
+        h3_scales = const.tile([P, PASSES * BATCH], U8, align_bytes=64)
+        h3_grouped = []
+        for c in range(2):
+            grouped = grouped_pool.tile([P, CHUNK, PACK], BF16, align_bytes=64)
+            h3_grouped.append(grouped)
+        for s in range(BATCH_TILES):
+            words = h3_raw[:, s, :].bitcast(F32).rearrange("p (g q u) -> p g u q", g=PASSES, u=2)
+            for c in range(2):
+                flipped = bank(2 * s + c, [P, 2, 2, P], F32)
+                for g2 in range(2):
+                    for u in range(2):
+                        nc.tensor.transpose(
+                            out=flipped[:, g2, u, :],
+                            in_=words[:, 2 * c + g2, u, :],
+                            identity=ident_f32[:],
+                        )
+                target = (
+                    h3_grouped[c][:]
+                    .rearrange("p w t -> p (w t)")
+                    .bitcast(F32)
+                    .rearrange("p (g b u) -> p g b u", g=2, u=2)
+                )
+                source = flipped[:].rearrange("p g u b -> p g b u")
+                if c == 0:
+                    nc.vector.tensor_copy(out=target[:, :, s * P : (s + 1) * P, :], in_=source)
+                else:
+                    nc.scalar.copy(out=target[:, :, s * P : (s + 1) * P, :], in_=source)
+
+        b4_t = bank(0, [P, P], BF16)
+        nc.tensor.transpose(out=b4_t[:], in_=b4_rows[:], identity=ident_bf16[:])
+        b4_cols = const.tile([P, MID // P], F32)
+        nc.vector.tensor_copy(out=b4_cols[:], in_=b4_t[:, 0 : MID // P])
+
+        fill(0)
+        for c in range(2):
+            cols = slice(c * CHUNK, (c + 1) * CHUNK)
+            quantise(nc, h3_codes[:, cols], h3_scales[:, cols], h3_grouped[c][:])
+
+        h4_planes = const.tile([P, MID // P, BATCH], BF16)
+        h4_codes = const.tile([P, PASSES * BATCH], U32, align_bytes=64)
+        h4_scales = const.tile([P, PASSES * BATCH], U8, align_bytes=64)
+        y_planes = const.tile([P, BANKS, 2, PAIRS], F32)
+
+        def x_planes(b):
+            h, s = divmod(b, BATCH_TILES)
+            return x_sb[:, s, h * BANK : (h + 1) * BANK].rearrange("p (c two) -> p two c", two=2)
+
+        def finish_half(half, acc):
+            for i in range(BANKS):
+                c = half * BANKS + i
+                if i % 2 == 0:
+                    nc.scalar.activation(
+                        out=h4_planes[:, c, :], in_=acc[i][:], func=ACT.Relu, bias=b4_cols[:, c : c + 1]
+                    )
+                else:
+                    nc.vector.tensor_scalar(
+                        out=h4_planes[:, c, :], in0=acc[i][:],
+                        scalar1=b4_cols[:, c : c + 1], scalar2=0.0, op0=ALU.add, op1=ALU.max,
+                    )
+            grouped = grouped_pool.tile([P, CHUNK, PACK], BF16, align_bytes=64)
+            for r2 in range(2):
+                first = half * BANKS + r2 * PACK
+                regroup(
+                    nc,
+                    grouped[:, r2 * BATCH : (r2 + 1) * BATCH, :],
+                    h4_planes[:, first : first + PACK, :],
+                )
+            return grouped
+
+        acc = None
+        for j in range(chunks):
+            if j + LOADS_AHEAD < chunks:
+                load(j + LOADS_AHEAD)
+            if j + 1 < chunks:
+                fill(j + 1)
+            stage, step = divmod(j, PASSES)
+            h4_grouped = None
+            if step == 0 and stage > 0:
+                h4_grouped = finish_half(stage - 1, acc)
+            w_codes, w_scales = quantise_chunk(j)
+            if h4_grouped is not None:
+                cols = slice((stage - 1) * CHUNK, stage * CHUNK)
+                quantise(nc, h4_codes[:, cols], h4_scales[:, cols], h4_grouped[:])
+            if step == 0:
+                acc = [bank(i, [P, BANK], F32) for i in range(BANKS)]
+            for i in range(BANKS):
+                if stage < 2:
+                    stationary, stationary_scales, m_cols = w_codes, w_scales, slice(i * P, (i + 1) * P)
+                    moving, moving_scales, n_cols = h3_codes, h3_scales, slice(step * BATCH, (step + 1) * BATCH)
+                else:
+                    h, s = divmod(i, BATCH_TILES)
+                    stationary, stationary_scales = h4_codes, h4_scales
+                    m_cols = slice(step * BATCH + s * P, step * BATCH + (s + 1) * P)
+                    moving, moving_scales, n_cols = w_codes, w_scales, slice(h * BANK, (h + 1) * BANK)
+                nc.tensor.matmul_mx(
+                    out=acc[i][:],
+                    lhsT=stationary[:, m_cols].bitcast(FP8X4),
+                    lhsT_scale=stationary_scales[:, m_cols],
+                    rhs=moving[:, n_cols].bitcast(FP8X4),
+                    rhs_scale=moving_scales[:, n_cols],
+                    start=(step == 0),
+                    stop=(step == PASSES - 1),
+                )
+            if stage == 2:
+                for b in (2 * step, 2 * step + 1):
+                    nc.scalar.copy(out=y_planes[:, b, 0, :], in_=x_planes(b)[:, 0, :])
+
+        ls_sums = const.tile([P, 2, BATCH_TILES], F32)
+        v_tiles, factor_tiles = [], []
+
+        def tail_front(b):
+            h, s = divmod(b, BATCH_TILES)
+            v_planes = tail_pool.tile([P, 2, PAIRS], F32)
+            nc.vector.tensor_tensor(
+                out=v_planes[:],
+                in0=acc[b][:].rearrange("p (c two) -> p two c", two=2),
+                in1=b5_all[:, h * BANK : (h + 1) * BANK].rearrange("p (c two) -> p two c", two=2),
+                op=ALU.add,
+            )
+            log_scale = tail_pool.tile([P, PAIRS], F32)
+            nc.scalar.activation(
+                out=log_scale[:], in_=v_planes[:, 0, :], func=ACT.Tanh,
+                accum_out=ls_sums[:, h, s : s + 1],
+            )
+            factor = tail_pool.tile([P, PAIRS], F32)
+            nc.scalar.activation(out=factor[:], in_=log_scale[:], func=ACT.Exp)
+            v_tiles.append(v_planes)
+            factor_tiles.append(factor)
+
+        def tail_back(b):
+            h, s = divmod(b, BATCH_TILES)
+            scaled = tail_pool.tile([P, PAIRS], F32)
+            nc.vector.tensor_tensor(
+                out=scaled[:], in0=x_planes(b)[:, 1, :], in1=factor_tiles[b][:], op=ALU.mult
+            )
+            nc.vector.tensor_tensor(
+                out=y_planes[:, b, 1, :], in0=scaled[:], in1=v_tiles[b][:, 1, :], op=ALU.add
+            )
+            y_sb = tail_pool.tile([P, BANK], F32)
+            nc.scalar.copy(
+                out=y_sb[:].rearrange("p (c two) -> p c two", two=2),
+                in_=y_planes[:, b, :, :].rearrange("p two c -> p c two"),
+            )
+            nc.sync.dma_start(out=out_0[s * P : (s + 1) * P, h * BANK : (h + 1) * BANK], in_=y_sb[:])
+
+        tail_front(0)
+        for b in range(1, BANKS):
+            tail_front(b)
+            tail_back(b - 1)
+        tail_back(BANKS - 1)
+
+        nc.vector.tensor_reduce(
+            out=ld_cols[:, 0:BATCH_TILES], in_=ls_sums[:].rearrange("p h s -> p s h"),
+            axis=mybir.AxisListType.X, op=ALU.add,
+        )
+        ld_t = bank(0, [P, P], F32)
+        nc.tensor.transpose(out=ld_t[:], in_=ld_cols[:], identity=ident_f32[:])
+        ld_rows = const.tile([P, P], F32)
+        nc.vector.tensor_tensor(out=ld_rows[:], in0=ld_t[:], in1=ldj_rows[:], op=ALU.add)
+        nc.sync.dma_start(out=out_1.rearrange("(s p) -> s p", p=P), in_=ld_rows[0:BATCH_TILES, :])

@@ -55,6 +55,7 @@ def tile_affinecoupling_pa_kernel(tc, h3, w4, b4, w5, b5, x, log_det_J, out_0, o
         const = ctx.enter_context(tc.tile_pool(name="const", bufs=1))
         raw_pool = ctx.enter_context(tc.tile_pool(name="raw", bufs=LOADS_AHEAD + 2))
         grouped_pool = ctx.enter_context(tc.tile_pool(name="grouped", bufs=4))
+        h3_pool = ctx.enter_context(tc.tile_pool(name="h3", bufs=2))
         weight_pool = ctx.enter_context(tc.tile_pool(name="weight", bufs=5))
         tail_pool = ctx.enter_context(tc.tile_pool(name="tail", bufs=3))
         psum = ctx.enter_context(tc.psum_pool(name="psum", bufs=1))
@@ -101,12 +102,12 @@ def tile_affinecoupling_pa_kernel(tc, h3, w4, b4, w5, b5, x, log_det_J, out_0, o
         raw_tiles, grouped_tiles = [], []
 
         def load(j):
-            if j == 2 * PASSES:
-                nc.sync.dma_start(out=x_sb[:], in_=x.rearrange("(s p) w -> p s w", p=P))
-                nc.sync.dma_start(out=b5_all[:], in_=b5.partition_broadcast(P))
             raw = raw_pool.tile([P, PACK, CHUNK], BF16)
             nc.sync.dma_start(out=raw[:], in_=chunk_rows[j])
             raw_tiles.append(raw)
+            if j == chunks - 1:
+                nc.sync.dma_start(out=x_sb[:], in_=x.rearrange("(s p) w -> p s w", p=P))
+                nc.sync.dma_start(out=b5_all[:], in_=b5.partition_broadcast(P))
 
         def fill(j):
             grouped = grouped_pool.tile([P, CHUNK, PACK], BF16, align_bytes=64)
@@ -125,12 +126,15 @@ def tile_affinecoupling_pa_kernel(tc, h3, w4, b4, w5, b5, x, log_det_J, out_0, o
 
         h3_codes = const.tile([P, PASSES * BATCH], U32, align_bytes=64)
         h3_scales = const.tile([P, PASSES * BATCH], U8, align_bytes=64)
-        h3_grouped = []
-        for c in range(2):
-            grouped = grouped_pool.tile([P, CHUNK, PACK], BF16, align_bytes=64)
-            h3_grouped.append(grouped)
         for s in range(BATCH_TILES):
             words = h3_raw[:, s, :].bitcast(F32).rearrange("p (g q u) -> p g u q", g=PASSES, u=2)
+            h3_grouped = h3_pool.tile([P, PASSES, P, PACK], BF16, align_bytes=64)
+            target = (
+                h3_grouped[:]
+                .rearrange("p g b t -> p (g b t)")
+                .bitcast(F32)
+                .rearrange("p (g b u) -> p g b u", g=PASSES, u=2)
+            )
             for c in range(2):
                 flipped = bank(2 * s + c, [P, 2, 2, P], F32)
                 for g2 in range(2):
@@ -140,17 +144,14 @@ def tile_affinecoupling_pa_kernel(tc, h3, w4, b4, w5, b5, x, log_det_J, out_0, o
                             in_=words[:, 2 * c + g2, u, :],
                             identity=ident_f32[:],
                         )
-                target = (
-                    h3_grouped[c][:]
-                    .rearrange("p w t -> p (w t)")
-                    .bitcast(F32)
-                    .rearrange("p (g b u) -> p g b u", g=2, u=2)
-                )
                 source = flipped[:].rearrange("p g u b -> p g b u")
                 if c == 0:
-                    nc.vector.tensor_copy(out=target[:, :, s * P : (s + 1) * P, :], in_=source)
+                    nc.vector.tensor_copy(out=target[:, 0:2, :, :], in_=source)
                 else:
-                    nc.scalar.copy(out=target[:, :, s * P : (s + 1) * P, :], in_=source)
+                    nc.scalar.copy(out=target[:, 2:4, :, :], in_=source)
+            for g in range(PASSES):
+                cols = slice(g * BATCH + s * P, g * BATCH + (s + 1) * P)
+                quantise(nc, h3_codes[:, cols], h3_scales[:, cols], h3_grouped[:, g, :, :])
 
         b4_t = bank(0, [P, P], BF16)
         nc.tensor.transpose(out=b4_t[:], in_=b4_rows[:], identity=ident_bf16[:])
@@ -158,9 +159,6 @@ def tile_affinecoupling_pa_kernel(tc, h3, w4, b4, w5, b5, x, log_det_J, out_0, o
         nc.vector.tensor_copy(out=b4_cols[:], in_=b4_t[:, 0 : MID // P])
 
         fill(0)
-        for c in range(2):
-            cols = slice(c * CHUNK, (c + 1) * CHUNK)
-            quantise(nc, h3_codes[:, cols], h3_scales[:, cols], h3_grouped[c][:])
 
         h4_planes = const.tile([P, MID // P, BATCH], BF16)
         h4_codes = const.tile([P, PASSES * BATCH], U32, align_bytes=64)
@@ -193,6 +191,34 @@ def tile_affinecoupling_pa_kernel(tc, h3, w4, b4, w5, b5, x, log_det_J, out_0, o
                 )
             return grouped
 
+        def stage1_passes(g, w_codes, w_scales, acc):
+            for i in range(BANKS):
+                nc.tensor.matmul_mx(
+                    out=acc[i][:],
+                    lhsT=w_codes[:, i * P : (i + 1) * P].bitcast(FP8X4),
+                    lhsT_scale=w_scales[:, i * P : (i + 1) * P],
+                    rhs=h3_codes[:, g * BATCH : (g + 1) * BATCH].bitcast(FP8X4),
+                    rhs_scale=h3_scales[:, g * BATCH : (g + 1) * BATCH],
+                    start=(g == 0),
+                    stop=(g == PASSES - 1),
+                )
+
+        w5_tiles = []
+
+        def stage2_passes(r, h, acc):
+            w_codes, w_scales = w5_tiles[r]
+            for s in range(BATCH_TILES):
+                rows_of_tile = slice(r * BATCH + s * P, r * BATCH + (s + 1) * P)
+                nc.tensor.matmul_mx(
+                    out=acc[BATCH_TILES * h + s][:],
+                    lhsT=h4_codes[:, rows_of_tile].bitcast(FP8X4),
+                    lhsT_scale=h4_scales[:, rows_of_tile],
+                    rhs=w_codes[:, h * BANK : (h + 1) * BANK].bitcast(FP8X4),
+                    rhs_scale=w_scales[:, h * BANK : (h + 1) * BANK],
+                    start=(r == 0),
+                    stop=(r == PASSES - 1),
+                )
+
         acc = None
         for j in range(chunks):
             if j + LOADS_AHEAD < chunks:
@@ -209,27 +235,22 @@ def tile_affinecoupling_pa_kernel(tc, h3, w4, b4, w5, b5, x, log_det_J, out_0, o
                 quantise(nc, h4_codes[:, cols], h4_scales[:, cols], h4_grouped[:])
             if step == 0:
                 acc = [bank(i, [P, BANK], F32) for i in range(BANKS)]
-            for i in range(BANKS):
-                if stage < 2:
-                    stationary, stationary_scales, m_cols = w_codes, w_scales, slice(i * P, (i + 1) * P)
-                    moving, moving_scales, n_cols = h3_codes, h3_scales, slice(step * BATCH, (step + 1) * BATCH)
+            if stage < 2:
+                stage1_passes(step, w_codes, w_scales, acc)
+            else:
+                w5_tiles.append((w_codes, w_scales))
+                if step < PASSES - 2:
+                    stage2_passes(step, 0, acc)
+                    stage2_passes(step, 1, acc)
+                elif step == PASSES - 2:
+                    stage2_passes(step, 0, acc)
                 else:
-                    h, s = divmod(i, BATCH_TILES)
-                    stationary, stationary_scales = h4_codes, h4_scales
-                    m_cols = slice(step * BATCH + s * P, step * BATCH + (s + 1) * P)
-                    moving, moving_scales, n_cols = w_codes, w_scales, slice(h * BANK, (h + 1) * BANK)
-                nc.tensor.matmul_mx(
-                    out=acc[i][:],
-                    lhsT=stationary[:, m_cols].bitcast(FP8X4),
-                    lhsT_scale=stationary_scales[:, m_cols],
-                    rhs=moving[:, n_cols].bitcast(FP8X4),
-                    rhs_scale=moving_scales[:, n_cols],
-                    start=(step == 0),
-                    stop=(step == PASSES - 1),
-                )
-            if stage == 2:
-                for b in (2 * step, 2 * step + 1):
-                    nc.scalar.copy(out=y_planes[:, b, 0, :], in_=x_planes(b)[:, 0, :])
+                    stage2_passes(step, 0, acc)
+                    stage2_passes(step - 1, 1, acc)
+                    stage2_passes(step, 1, acc)
+
+        for b in range(BANKS):
+            nc.scalar.copy(out=y_planes[:, b, 0, :], in_=x_planes(b)[:, 0, :])
 
         ls_sums = const.tile([P, 2, BATCH_TILES], F32)
         v_tiles, factor_tiles = [], []

@@ -25,18 +25,13 @@ CHUNK = 1024
 PAIRS = BANK // 2
 RUN = 4
 LOADS_AHEAD = 5
+VECTOR_COLS = CHUNK * 9 // 16
 
 
-def regroup(nc, grouped, planes):
-    width = planes.shape[2]
-    half = width // 2
-    nc.vector.tensor_copy(
-        out=grouped[:, 0:half, :].rearrange("p (c i) t -> p c t i", i=RUN),
-        in_=planes[:, :, 0:half].rearrange("p t (c i) -> p c t i", i=RUN),
-    )
-    nc.scalar.copy(
-        out=grouped[:, half:width, :].rearrange("p (c i) t -> p c t i", i=RUN),
-        in_=planes[:, :, half:width].rearrange("p t (c i) -> p c t i", i=RUN),
+def regroup(copy, grouped, planes):
+    copy(
+        out=grouped.rearrange("p (c i) t -> p c t i", i=RUN),
+        in_=planes.rearrange("p t (c i) -> p c t i", i=RUN),
     )
 
 
@@ -111,7 +106,9 @@ def tile_affinecoupling_pa_kernel(tc, h3, w4, b4, w5, b5, x, log_det_J, out_0, o
 
         def fill(j):
             grouped = grouped_pool.tile([P, CHUNK, PACK], BF16, align_bytes=64)
-            regroup(nc, grouped, raw_tiles[j])
+            raw = raw_tiles[j]
+            regroup(nc.vector.tensor_copy, grouped[:, 0:VECTOR_COLS, :], raw[:, :, 0:VECTOR_COLS])
+            regroup(nc.scalar.copy, grouped[:, VECTOR_COLS:CHUNK, :], raw[:, :, VECTOR_COLS:CHUNK])
             grouped_tiles.append(grouped)
 
         def quantise_chunk(j):
@@ -169,23 +166,19 @@ def tile_affinecoupling_pa_kernel(tc, h3, w4, b4, w5, b5, x, log_det_J, out_0, o
             h, s = divmod(b, BATCH_TILES)
             return x_sb[:, s, h * BANK : (h + 1) * BANK].rearrange("p (c two) -> p two c", two=2)
 
-        def finish_half(half, acc):
+        def leave_psum(half, acc):
             for i in range(BANKS):
                 c = half * BANKS + i
-                if i % 2 == 0:
-                    nc.scalar.activation(
-                        out=h4_planes[:, c, :], in_=acc[i][:], func=ACT.Relu, bias=b4_cols[:, c : c + 1]
-                    )
-                else:
-                    nc.vector.tensor_scalar(
-                        out=h4_planes[:, c, :], in0=acc[i][:],
-                        scalar1=b4_cols[:, c : c + 1], scalar2=0.0, op0=ALU.add, op1=ALU.max,
-                    )
+                nc.scalar.activation(
+                    out=h4_planes[:, c, :], in_=acc[i][:], func=ACT.Relu, bias=b4_cols[:, c : c + 1]
+                )
+
+        def regroup_h4(half):
             grouped = grouped_pool.tile([P, CHUNK, PACK], BF16, align_bytes=64)
             for r2 in range(2):
                 first = half * BANKS + r2 * PACK
                 regroup(
-                    nc,
+                    nc.vector.tensor_copy,
                     grouped[:, r2 * BATCH : (r2 + 1) * BATCH, :],
                     h4_planes[:, first : first + PACK, :],
                 )
@@ -228,7 +221,9 @@ def tile_affinecoupling_pa_kernel(tc, h3, w4, b4, w5, b5, x, log_det_J, out_0, o
             stage, step = divmod(j, PASSES)
             h4_grouped = None
             if step == 0 and stage > 0:
-                h4_grouped = finish_half(stage - 1, acc)
+                leave_psum(stage - 1, acc)
+            if step == 1 and stage > 0:
+                h4_grouped = regroup_h4(stage - 1)
             w_codes, w_scales = quantise_chunk(j)
             if h4_grouped is not None:
                 cols = slice((stage - 1) * CHUNK, stage * CHUNK)

@@ -173,7 +173,7 @@ def tile_affinecoupling_pa_kernel(tc, h3, w4, b4, w5, b5, x, log_det_J, out_0, o
                     out=h4_planes[:, c, :], in_=acc[i][:], func=ACT.Relu, bias=b4_cols[:, c : c + 1]
                 )
 
-        def regroup_h4(half):
+        def quantise_h4(half):
             grouped = grouped_pool.tile([P, CHUNK, PACK], BF16, align_bytes=64)
             for r2 in range(2):
                 first = half * BANKS + r2 * PACK
@@ -182,7 +182,13 @@ def tile_affinecoupling_pa_kernel(tc, h3, w4, b4, w5, b5, x, log_det_J, out_0, o
                     grouped[:, r2 * BATCH : (r2 + 1) * BATCH, :],
                     h4_planes[:, first : first + PACK, :],
                 )
-            return grouped
+            for r2 in range(2):
+                r = 2 * half + r2
+                cols = slice(r * BATCH, (r + 1) * BATCH)
+                quantise(
+                    nc, h4_codes[:, cols], h4_scales[:, cols],
+                    grouped[:, r2 * BATCH : (r2 + 1) * BATCH, :],
+                )
 
         def stage1_passes(g, w_codes, w_scales, acc):
             for i in range(BANKS):
@@ -219,15 +225,11 @@ def tile_affinecoupling_pa_kernel(tc, h3, w4, b4, w5, b5, x, log_det_J, out_0, o
             if j + 1 < chunks:
                 fill(j + 1)
             stage, step = divmod(j, PASSES)
-            h4_grouped = None
             if step == 0 and stage > 0:
                 leave_psum(stage - 1, acc)
-            if step == 1 and stage > 0:
-                h4_grouped = regroup_h4(stage - 1)
+            if step == 2 and stage > 0:
+                quantise_h4(stage - 1)
             w_codes, w_scales = quantise_chunk(j)
-            if h4_grouped is not None:
-                cols = slice((stage - 1) * CHUNK, stage * CHUNK)
-                quantise(nc, h4_codes[:, cols], h4_scales[:, cols], h4_grouped[:])
             if step == 0:
                 acc = [bank(i, [P, BANK], F32) for i in range(BANKS)]
             if stage < 2:
@@ -289,7 +291,6 @@ def tile_affinecoupling_pa_kernel(tc, h3, w4, b4, w5, b5, x, log_det_J, out_0, o
         for b in range(1, BANKS):
             tail_front(b)
             tail_back(b - 1)
-        tail_back(BANKS - 1)
 
         nc.vector.tensor_reduce(
             out=ld_cols[:, 0:BATCH_TILES], in_=ls_sums[:].rearrange("p h s -> p s h"),
@@ -297,6 +298,7 @@ def tile_affinecoupling_pa_kernel(tc, h3, w4, b4, w5, b5, x, log_det_J, out_0, o
         )
         ld_t = bank(0, [P, P], F32)
         nc.tensor.transpose(out=ld_t[:], in_=ld_cols[:], identity=ident_f32[:])
+        tail_back(BANKS - 1)
         ld_rows = const.tile([P, P], F32)
         nc.vector.tensor_tensor(out=ld_rows[:], in0=ld_t[:], in1=ldj_rows[:], op=ALU.add)
         nc.sync.dma_start(out=out_1.rearrange("(s p) -> s p", p=P), in_=ld_rows[0:BATCH_TILES, :])

from contextlib import ExitStack

import concourse.mybir as mybir
from concourse.masks import make_identity

F32 = mybir.dt.float32
BF16 = mybir.dt.bfloat16
U32 = mybir.dt.uint32
U8 = mybir.dt.uint8
FP8X4 = mybir.dt.float8_e4m3fn_x4
ACT = mybir.ActivationFunctionType
ALU = mybir.AluOpType

BATCH, MID, WIDTH = 512, 2048, 1024
FLOPS = 2 * BATCH * MID * MID + 2 * BATCH * MID * WIDTH

P = 128
PACK = 4
K_PASS = P * PACK
PASSES = MID // K_PASS
BATCH_TILES = BATCH // P
BANK = 512
BANKS = 8
CHUNK = 1024
PAIRS = BANK // 2
RUN = 4
LOADS_AHEAD = 5
VECTOR_COLS = CHUNK * 9 // 16


def regroup(copy, grouped, planes):
    copy(
        out=grouped.rearrange("p (c i) t -> p c t i", i=RUN),
        in_=planes.rearrange("p t (c i) -> p c t i", i=RUN),
    )


def quantise(nc, codes, scales, grouped):
    nc.vector.quantize_mx(
        out=codes.bitcast(FP8X4),
        scales=scales,
        in_=grouped.rearrange("p w t -> p (w t)"),
    )


def tile_affinecoupling_pa_kernel(tc, h3, w4, b4, w5, b5, x, log_det_J, out_0, out_1):
    nc = tc.nc
    with ExitStack() as ctx:
        ctx.enter_context(tc.manual_schedule())
        const = ctx.enter_context(tc.tile_pool(name="const", bufs=1))
        raw_pool = ctx.enter_context(tc.tile_pool(name="raw", bufs=LOADS_AHEAD + 2))
        grouped_pool = ctx.enter_context(tc.tile_pool(name="grouped", bufs=4))
        h3_pool = ctx.enter_context(tc.tile_pool(name="h3", bufs=2))
        weight_pool = ctx.enter_context(tc.tile_pool(name="weight", bufs=5))
        tail_pool = ctx.enter_context(tc.tile_pool(name="tail", bufs=3))
        psum = ctx.enter_context(tc.psum_pool(name="psum", bufs=1))

        def bank(i, shape, dtype):
            return psum.tile(shape, dtype, name="bank%d" % i)

        ident_f32 = const.tile([P, P], F32)
        make_identity(nc, ident_f32[:])
        ident_bf16 = const.tile([P, P], BF16)
        make_identity(nc, ident_bf16[:])

        warm = const.tile([P, 1], F32)
        nc.vector.memset(warm[:], 0.0)
        nc.scalar.activation(out=warm[:], in_=warm[:], func=ACT.Tanh)

        b4_rows = const.tile([P, P], BF16)
        nc.vector.memset(b4_rows[:], 0.0)
        nc.scalar.dma_start(out=b4_rows[0 : MID // P, :], in_=b4.rearrange("(c p) -> c p", p=P))
        ldj_rows = const.tile([P, P], BF16)
        nc.vector.memset(ldj_rows[:], 0.0)
        nc.scalar.dma_start(
            out=ldj_rows[0:BATCH_TILES, :], in_=log_det_J.rearrange("(s p) -> s p", p=P)
        )
        ld_cols = const.tile([P, P], F32)
        nc.vector.memset(ld_cols[:], 0.0)

        h3_raw = const.tile([P, BATCH_TILES, MID], BF16)
        for s in range(BATCH_TILES):
            nc.sync.dma_start(out=h3_raw[:, s, :], in_=h3[s * P : (s + 1) * P, :])

        x_sb = const.tile([P, BATCH_TILES, WIDTH], BF16)
        b5_all = const.tile([P, WIDTH], BF16)

        chunk_rows = []
        for half in range(2):
            for g in range(PASSES):
                rows = w4[g * K_PASS : (g + 1) * K_PASS, half * CHUNK : (half + 1) * CHUNK]
                chunk_rows.append(rows.rearrange("(p t) n -> p t n", t=PACK))
        for r in range(PASSES):
            rows = w5[r * K_PASS : (r + 1) * K_PASS, :]
            chunk_rows.append(rows.rearrange("(t p) n -> p t n", p=P))
        chunks = len(chunk_rows)
        raw_tiles, grouped_tiles = [], []

        def load(j):
            raw = raw_pool.tile([P, PACK, CHUNK], BF16)
            nc.sync.dma_start(out=raw[:], in_=chunk_rows[j])
            raw_tiles.append(raw)
            if j == chunks - 1:
                nc.sync.dma_start(out=x_sb[:], in_=x.rearrange("(s p) w -> p s w", p=P))
                nc.sync.dma_start(out=b5_all[:], in_=b5.partition_broadcast(P))

        def fill(j):
            grouped = grouped_pool.tile([P, CHUNK, PACK], BF16, align_bytes=64)
            raw = raw_tiles[j]
            regroup(nc.vector.tensor_copy, grouped[:, 0:VECTOR_COLS, :], raw[:, :, 0:VECTOR_COLS])
            regroup(nc.scalar.copy, grouped[:, VECTOR_COLS:CHUNK, :], raw[:, :, VECTOR_COLS:CHUNK])
            grouped_tiles.append(grouped)

        def quantise_chunk(j):
            w_codes = weight_pool.tile([P, CHUNK], U32, align_bytes=64)
            w_scales = weight_pool.tile([P, CHUNK], U8, align_bytes=64)
            for cols in (slice(0, BANK), slice(BANK, CHUNK)):
                quantise(nc, w_codes[:, cols], w_scales[:, cols], grouped_tiles[j][:, cols, :])
            return w_codes, w_scales

        for j in range(LOADS_AHEAD):
            load(j)

        h3_codes = const.tile([P, PASSES * BATCH], U32, align_bytes=64)
        h3_scales = const.tile([P, PASSES * BATCH], U8, align_bytes=64)
        for s in range(BATCH_TILES):
            words = h3_raw[:, s, :].bitcast(F32).rearrange("p (g q u) -> p g u q", g=PASSES, u=2)
            h3_grouped = h3_pool.tile([P, PASSES, P, PACK], BF16, align_bytes=64)
            target = (
                h3_grouped[:]
                .rearrange("p g b t -> p (g b t)")
                .bitcast(F32)
                .rearrange("p (g b u) -> p g b u", g=PASSES, u=2)
            )
            for c in range(2):
                flipped = bank(2 * s + c, [P, 2, 2, P], F32)
                for g2 in range(2):
                    for u in range(2):
                        nc.tensor.transpose(
                            out=flipped[:, g2, u, :],
                            in_=words[:, 2 * c + g2, u, :],
                            identity=ident_f32[:],
                        )
                source = flipped[:].rearrange("p g u b -> p g b u")
                if c == 0:
                    nc.vector.tensor_copy(out=target[:, 0:2, :, :], in_=source)
                else:
                    nc.scalar.copy(out=target[:, 2:4, :, :], in_=source)
            for g in range(PASSES):
                cols = slice(g * BATCH + s * P, g * BATCH + (s + 1) * P)
                quantise(nc, h3_codes[:, cols], h3_scales[:, cols], h3_grouped[:, g, :, :])

        b4_t = bank(0, [P, P], BF16)
        nc.tensor.transpose(out=b4_t[:], in_=b4_rows[:], identity=ident_bf16[:])
        b4_cols = const.tile([P, MID // P], F32)
        nc.vector.tensor_copy(out=b4_cols[:], in_=b4_t[:, 0 : MID // P])

        fill(0)

        h4_planes = const.tile([P, MID // P, BATCH], BF16)
        h4_codes = const.tile([P, PASSES * BATCH], U32, align_bytes=64)
        h4_scales = const.tile([P, PASSES * BATCH], U8, align_bytes=64)
        y_planes = const.tile([P, BANKS, 2, PAIRS], F32)

        def x_planes(b):
            h, s = divmod(b, BATCH_TILES)
            return x_sb[:, s, h * BANK : (h + 1) * BANK].rearrange("p (c two) -> p two c", two=2)

        def leave_psum(half, acc):
            for i in range(BANKS):
                c = half * BANKS + i
                nc.scalar.activation(
                    out=h4_planes[:, c, :], in_=acc[i][:], func=ACT.Relu, bias=b4_cols[:, c : c + 1]
                )

        def quantise_h4(half):
            grouped = grouped_pool.tile([P, CHUNK, PACK], BF16, align_bytes=64)
            for r2 in range(2):
                first = half * BANKS + r2 * PACK
                regroup(
                    nc.vector.tensor_copy,
                    grouped[:, r2 * BATCH : (r2 + 1) * BATCH, :],
                    h4_planes[:, first : first + PACK, :],
                )
            for r2 in range(2):
                r = 2 * half + r2
                cols = slice(r * BATCH, (r + 1) * BATCH)
                quantise(
                    nc, h4_codes[:, cols], h4_scales[:, cols],
                    grouped[:, r2 * BATCH : (r2 + 1) * BATCH, :],
                )

        def stage1_passes(g, w_codes, w_scales, acc):
            for i in range(BANKS):
                nc.tensor.matmul_mx(
                    out=acc[i][:],
                    lhsT=w_codes[:, i * P : (i + 1) * P].bitcast(FP8X4),
                    lhsT_scale=w_scales[:, i * P : (i + 1) * P],
                    rhs=h3_codes[:, g * BATCH : (g + 1) * BATCH].bitcast(FP8X4),
                    rhs_scale=h3_scales[:, g * BATCH : (g + 1) * BATCH],
                    start=(g == 0),
                    stop=(g == PASSES - 1),
                )

        w5_tiles = []

        def stage2_passes(r, h, acc):
            w_codes, w_scales = w5_tiles[r]
            for s in range(BATCH_TILES):
                rows_of_tile = slice(r * BATCH + s * P, r * BATCH + (s + 1) * P)
                nc.tensor.matmul_mx(
                    out=acc[BATCH_TILES * h + s][:],
                    lhsT=h4_codes[:, rows_of_tile].bitcast(FP8X4),
                    lhsT_scale=h4_scales[:, rows_of_tile],
                    rhs=w_codes[:, h * BANK : (h + 1) * BANK].bitcast(FP8X4),
                    rhs_scale=w_scales[:, h * BANK : (h + 1) * BANK],
                    start=(r == 0),
                    stop=(r == PASSES - 1),
                )

        acc = None
        for j in range(chunks):
            if j + LOADS_AHEAD < chunks:
                load(j + LOADS_AHEAD)
            if j + 1 < chunks:
                fill(j + 1)
            stage, step = divmod(j, PASSES)
            if step == 0 and stage > 0:
                leave_psum(stage - 1, acc)
            if step == 2 and stage > 0:
                quantise_h4(stage - 1)
            w_codes, w_scales = quantise_chunk(j)
            if step == 0:
                acc = [bank(i, [P, BANK], F32) for i in range(BANKS)]
            if stage < 2:
                stage1_passes(step, w_codes, w_scales, acc)
            else:
                w5_tiles.append((w_codes, w_scales))
                if step < PASSES - 2:
                    stage2_passes(step, 0, acc)
                    stage2_passes(step, 1, acc)
                elif step == PASSES - 2:
                    stage2_passes(step, 0, acc)
                else:
                    stage2_passes(step, 0, acc)
                    stage2_passes(step - 1, 1, acc)
                    stage2_passes(step, 1, acc)

        for b in range(BANKS):
            nc.scalar.copy(out=y_planes[:, b, 0, :], in_=x_planes(b)[:, 0, :])

        ls_sums = const.tile([P, 2, BATCH_TILES], F32)
        v_tiles, factor_tiles = [], []

        def tail_front(b):
            h, s = divmod(b, BATCH_TILES)
            v_planes = tail_pool.tile([P, 2, PAIRS], F32)
            nc.vector.tensor_tensor(
                out=v_planes[:],
                in0=acc[b][:].rearrange("p (c two) -> p two c", two=2),
                in1=b5_all[:, h * BANK : (h + 1) * BANK].rearrange("p (c two) -> p two c", two=2),
                op=ALU.add,
            )
            log_scale = tail_pool.tile([P, PAIRS], F32)
            nc.scalar.activation(
                out=log_scale[:], in_=v_planes[:, 0, :], func=ACT.Tanh,
                accum_out=ls_sums[:, h, s : s + 1],
            )
            factor = tail_pool.tile([P, PAIRS], F32)
            nc.scalar.activation(out=factor[:], in_=log_scale[:], func=ACT.Exp)
            v_tiles.append(v_planes)
            factor_tiles.append(factor)

        def tail_back(b):
            h, s = divmod(b, BATCH_TILES)
            scaled = tail_pool.tile([P, PAIRS], F32)
            nc.vector.tensor_tensor(
                out=scaled[:], in0=x_planes(b)[:, 1, :], in1=factor_tiles[b][:], op=ALU.mult
            )
            nc.vector.tensor_tensor(
                out=y_planes[:, b, 1, :], in0=scaled[:], in1=v_tiles[b][:, 1, :], op=ALU.add
            )
            y_sb = tail_pool.tile([P, BANK], F32)
            nc.scalar.copy(
                out=y_sb[:].rearrange("p (c two) -> p c two", two=2),
                in_=y_planes[:, b, :, :].rearrange("p two c -> p c two"),
            )
            nc.sync.dma_start(out=out_0[s * P : (s + 1) * P, h * BANK : (h + 1) * BANK], in_=y_sb[:])

        tail_front(0)
        for b in range(1, BANKS):
            tail_front(b)
            tail_back(b - 1)

        nc.vector.tensor_reduce(
            out=ld_cols[:, 0:BATCH_TILES], in_=ls_sums[:].rearrange("p h s -> p s h"),
            axis=mybir.AxisListType.X, op=ALU.add,
        )
        ld_t = bank(0, [P, P], F32)
        nc.tensor.transpose(out=ld_t[:], in_=ld_cols[:], identity=ident_f32[:])
        tail_back(BANKS - 1)
        ld_rows = const.tile([P, P], F32)
        nc.vector.tensor_tensor(out=ld_rows[:], in0=ld_t[:], in1=ldj_rows[:], op=ALU.add)
        nc.sync.dma_start(out=out_1.rearrange("(s p) -> s p", p=P), in_=ld_rows[0:BATCH_TILES, :])
